import numpy as np
import ml_dtypes


def mxq(x, axis, fmt="e4m3"):
    dtype, down = {"e4m3": (ml_dtypes.float8_e4m3fn, 7), "e5m2": (ml_dtypes.float8_e5m2, 14)}[fmt]
    v = np.moveaxis(np.asarray(x, np.float32).astype(ml_dtypes.bfloat16).astype(np.float64), axis, -1)
    blocks = v.reshape(v.shape[:-1] + (-1, 32))
    amax = np.abs(blocks).max(-1, keepdims=True)
    byte = np.maximum(np.where(amax > 0, np.frexp(amax)[1] - 1 + 127, 0) - down, 1)
    scale = np.exp2(byte - 127.0)
    codes = (blocks / scale).astype(np.float32).astype(dtype).astype(np.float64)
    return np.moveaxis((codes * scale).reshape(v.shape), -1, axis)


WIDE = False


def mx_kscale(k):
    if not WIDE:
        return np.ones(k)
    levels = np.array([10, -10, 5, -5, 0])
    if k % 512:
        return np.exp2(np.random.permutation(np.resize(levels, k // 32))).repeat(32)
    a = np.empty((k // 512, 16))
    for p in range(k // 512):
        a[p, :8] = np.random.permutation(np.resize(levels, 8))
        for g in range(8):
            far = levels[np.abs(levels - a[p, g]) >= 10]
            a[p, g + 8] = far[np.random.randint(len(far))]
    return np.exp2(a.ravel()).repeat(32)


BF16 = ml_dtypes.bfloat16


def bf(x):
    return np.asarray(x, np.float32).astype(BF16)


def f64(x):
    return np.asarray(x).astype(np.float64)


B, IMG, P0, P1, C, F = 2, 512, 8, 16, 2, 512
E0, E1 = IMG // P0, IMG // P1
N0, N1 = E0 * E0, E1 * E1
D0, D1 = P0 * P0 * C, P1 * P1 * C


def setup_inputs():
    s = mx_kscale(D1)
    flat = np.random.standard_normal((B, N1, D1)) * s
    img = flat.reshape(B, E1, E1, P1, P1, C).transpose(0, 1, 3, 2, 4, 5).reshape(B, IMG, IMG, C)
    encoded = img.reshape(B, E0, P0, E0, P0, C).transpose(0, 1, 3, 2, 4, 5).reshape(B, N0, D0)
    return {"encoded": bf(encoded),
            "W": bf(np.random.standard_normal((D1, F)) / np.sqrt(D1) / s[:, None]),
            "b": bf(np.random.standard_normal(F) * 0.3),
            "pos_emb": bf(np.random.standard_normal((N1, F)) * 0.5)}


def reference(encoded, W, b, pos_emb):
    x = f64(encoded).reshape(-1, E0, E0, P0, P0, C)
    img = x.transpose(0, 1, 3, 2, 4, 5).reshape(-1, IMG, IMG, C)
    new_patches = img.reshape(-1, E1, P1, E1, P1, C).transpose(0, 1, 3, 2, 4, 5)
    flat = new_patches.reshape(-1, N1, D1)
    return (mxq(flat, 2, "e4m3") @ mxq(f64(W), 0, "e4m3")) + f64(b) + f64(pos_emb)

@@ -1,0 +1,186 @@
+from contextlib import ExitStack
+
+import concourse.mybir as mybir
+from concourse.masks import make_identity
+
+F32 = mybir.dt.float32
+BF16 = mybir.dt.bfloat16
+I32 = mybir.dt.int32
+U32 = mybir.dt.uint32
+U8 = mybir.dt.uint8
+FP8X4 = mybir.dt.float8_e4m3fn_x4
+ADD = mybir.AluOpType.add
+
+P = 128
+F = 512
+FLOPS = 2 * 2048 * 512 * 512
+
+
+def tile_resampling_kernel(tc, encoded, W, b, pos_emb, out):
+    nc = tc.nc
+    with ExitStack() as ctx:
+        const = ctx.enter_context(tc.tile_pool(name="const", bufs=1))
+        ps_t = ctx.enter_context(tc.psum_pool(name="ps_t", bufs=3))
+        ps_o = ctx.enter_context(tc.psum_pool(name="ps_o", bufs=4))
+        ctx.enter_context(tc.manual_schedule())
+
+        enc_v = encoded.rearrange("i (Y y C c) d -> i Y C y (c d)", Y=32, y=2, C=4)
+        w_v = W.rearrange("(y h w e) f -> h y w (e f)", y=16, h=2, w=8, e=2)
+        pos_v = pos_emb.rearrange("(m x) f -> m x f", x=8)
+        out_v = out.rearrange("i (m x) f -> i m x f", x=8)
+        chunks = [(0, 0), (1, 0), (0, 1), (1, 1)]
+
+        brow = const.tile([P, F], BF16, name="brow")
+        nc.vector.memset(brow[:], 0.0)
+        ones = const.tile([P, P], BF16, name="ones")
+        nc.vector.memset(ones[:], 1.0)
+        ident = const.tile([P, P], F32, name="ident")
+        make_identity(nc, ident[:])
+
+        w_raw = const.tile([P, 4, F], BF16, name="w_raw")
+        pos = const.tile([P, 8, F], BF16, name="pos")
+        enc_sb = [const.tile([P, 2, 1024], BF16, name="enc%d" % c) for c in range(4)]
+
+        def load_w(h):
+            nc.sync.dma_start(out=w_raw[:, 2 * h:2 * h + 2, :].rearrange("s c f -> s (c f)"),
+                              in_=w_v[h])
+
+        def load_enc(c):
+            i, h = chunks[c]
+            for y in range(2):
+                nc.sync.dma_start(out=enc_sb[c][:, y, :],
+                                  in_=enc_v[i][:, :, y, h * 1024:(h + 1) * 1024])
+
+        def load_pos(h):
+            nc.sync.dma_start(out=pos[:, 4 * h:4 * h + 4, :], in_=pos_v[:, 4 * h:4 * h + 4, :])
+
+        load_w(0)
+        nc.sync.dma_start(out=brow[0:1, :], in_=b.rearrange("(o f) -> o f", o=1))
+        load_w(1)
+        load_enc(0)
+        load_pos(0)
+        load_enc(1)
+        load_pos(1)
+        load_enc(2)
+        load_enc(3)
+
+        w_grp = const.tile([P, F, 4], BF16, name="w_grp", align_bytes=64)
+        w_codes = const.tile([P, F], U32, name="w_codes", align_bytes=64)
+        w_scales = const.tile([P, F], U8, name="w_scales", align_bytes=64)
+        bbc = const.tile([P, F], BF16, name="bbc")
+        pb = ps_t.tile([P, F], F32, name="pb", tag="t")
+        nc.tensor.matmul(out=pb[:], lhsT=ones[:], rhs=brow[:], start=True, stop=True)
+        nc.scalar.copy(out=bbc[:], in_=pb[:])
+
+        def regroup_w(copy, c0, c1):
+            copy(out=w_grp[:, c0:c1, :].rearrange("p (c i) t -> p c t i", i=4),
+                 in_=w_raw[:, :, c0:c1].rearrange("p t (c i) -> p c t i", i=4))
+
+        regroup_w(nc.scalar.copy, 336, 512)
+        regroup_w(nc.vector.tensor_copy, 0, 256)
+        regroup_w(nc.vector.tensor_copy, 256, 336)
+        for k in range(2):
+            nc.vector.quantize_mx(out=w_codes[:, k * 256:(k + 1) * 256].bitcast(FP8X4),
+                                  scales=w_scales[:, k * 256:(k + 1) * 256],
+                                  in_=w_grp[:, k * 256:(k + 1) * 256, :].rearrange("p f t -> p (f t)"))
+
+        posb = const.tile([P, 8, F], F32, name="posb")
+
+        def add_bias(eng, x):
+            eng.tensor_tensor(out=posb[:, x, :], in0=pos[:, x, :], in1=bbc[:], op=ADD)
+
+        for x in range(1, 8):
+            add_bias(nc.gpsimd, x)
+
+        grp = [const.tile([P, 2048], BF16, name="grp%d" % c, align_bytes=64) for c in range(4)]
+        codes = [const.tile([P, F], U32, name="codes%d" % c, align_bytes=64) for c in range(4)]
+        scales = [const.tile([P, F], U8, name="scales%d" % c, align_bytes=64) for c in range(4)]
+        res = [const.tile([P, 4, F], F32, name="res%d" % c) for c in range(4)]
+
+        ord_sb = [const.tile([P, 1024], F32, name="ord%d" % c) for c in range(4)]
+
+        def reorder(u, copy):
+            c, bank = u // 2, u % 2
+            copy(out=ord_sb[c][:, bank * F:(bank + 1) * F].rearrange("p (u y w) -> p u y w", u=4, y=2),
+                 in_=enc_sb[c][:].bitcast(F32)[:, :, bank * 256:(bank + 1) * 256]
+                 .rearrange("p y (u w) -> p u y w", u=4))
+
+        def transpose_unit(u):
+            c, bank = u // 2, u % 2
+            pt = ps_t.tile([P, F], F32, name="pt", tag="t")
+            for s in range(4):
+                nc.tensor.transpose(pt[:, s * P:(s + 1) * P],
+                                    ord_sb[c][:, (4 * bank + s) * P:(4 * bank + s + 1) * P], ident[:])
+            return pt
+
+        def evacuate(u, pt):
+            c, bank = u // 2, u % 2
+            nc.scalar.copy(
+                out=grp[c][:].bitcast(F32)[:, bank * F:(bank + 1) * F]
+                .rearrange("p (x q h) -> p x q h", x=2, h=2),
+                in_=pt[:].rearrange("p (x h q) -> p x q h", x=2, h=2))
+
+        def transpose_pair(u):
+            banks = [transpose_unit(u), transpose_unit(u + 1)]
+            evacuate(u, banks[0])
+            evacuate(u + 1, banks[1])
+
+        def quantise(u):
+            c, bank = u // 2, u % 2
+            nc.vector.quantize_mx(
+                out=codes[c][:, bank * 256:(bank + 1) * 256].bitcast(FP8X4),
+                scales=scales[c][:, bank * 256:(bank + 1) * 256],
+                in_=grp[c][:, bank * 1024:(bank + 1) * 1024],
+            )
+
+        def mx_pass(n):
+            c, xi = n // 4, n % 4
+            po = ps_o.tile([P, F], F32, name="po", tag="o")
+            nc.tensor.matmul_mx(
+                out=po[:],
+                lhsT=codes[c][:, xi * P:(xi + 1) * P].bitcast(FP8X4),
+                lhsT_scale=scales[c][:, xi * P:(xi + 1) * P],
+                rhs=w_codes[:].bitcast(FP8X4),
+                rhs_scale=w_scales[:],
+                start=True,
+                stop=True,
+            )
+            return po
+
+        def finish(n, po):
+            c, xi = n // 4, n % 4
+            i, h = chunks[c]
+            nc.vector.tensor_tensor(out=res[c][:, xi, :], in0=po[:], in1=posb[:, h * 4 + xi, :],
+                                    op=ADD)
+            nc.sync.dma_start(out=out_v[i][:, h * 4 + xi, :], in_=res[c][:, xi, :])
+
+        def finish_unit(u, acc):
+            finish(2 * u, acc[0])
+            finish(2 * u + 1, acc[1])
+            if u + 2 < 8:
+                quantise(u + 2)
+
+        reorder(0, nc.vector.tensor_copy)
+        reorder(1, nc.vector.tensor_copy)
+        transpose_pair(0)
+        reorder(2, nc.scalar.copy)
+        reorder(3, nc.scalar.copy)
+        quantise(0)
+        add_bias(nc.vector, 0)
+        quantise(1)
+        first = [mx_pass(0), mx_pass(1)]
+        transpose_pair(2)
+        reorder(4, nc.scalar.copy)
+        reorder(5, nc.scalar.copy)
+        second = [mx_pass(2), mx_pass(3)]
+        finish_unit(0, first)
+        finish_unit(1, second)
+        for g in range(1, 4):
+            if g < 3:
+                transpose_pair(2 * g + 2)
+                if g < 2:
+                    reorder(6, nc.scalar.copy)
+                    reorder(7, nc.scalar.copy)
+            acc = [mx_pass(4 * g + k) for k in range(4)]
+            finish_unit(2 * g, acc[0:2])
+            finish_unit(2 * g + 1, acc[2:4])

@@ -5,7 +5,6 @@ from concourse.masks import make_identity
 
 F32 = mybir.dt.float32
 BF16 = mybir.dt.bfloat16
-I32 = mybir.dt.int32
 U32 = mybir.dt.uint32
 U8 = mybir.dt.uint8
 FP8X4 = mybir.dt.float8_e4m3fn_x4
@@ -21,7 +20,7 @@ def tile_resampling_kernel(tc, encoded, W, b, pos_emb, out):
     with ExitStack() as ctx:
         const = ctx.enter_context(tc.tile_pool(name="const", bufs=1))
         ps_t = ctx.enter_context(tc.psum_pool(name="ps_t", bufs=3))
-        ps_o = ctx.enter_context(tc.psum_pool(name="ps_o", bufs=4))
+        ps_o = ctx.enter_context(tc.psum_pool(name="ps_o", bufs=5))
         ctx.enter_context(tc.manual_schedule())
 
         enc_v = encoded.rearrange("i (Y y C c) d -> i Y C y (c d)", Y=32, y=2, C=4)
@@ -31,73 +30,54 @@ def tile_resampling_kernel(tc, encoded, W, b, pos_emb, out):
         chunks = [(0, 0), (1, 0), (0, 1), (1, 1)]
 
         brow = const.tile([P, F], BF16, name="brow")
-        nc.vector.memset(brow[:], 0.0)
         ones = const.tile([P, P], BF16, name="ones")
-        nc.vector.memset(ones[:], 1.0)
         ident = const.tile([P, P], F32, name="ident")
-        make_identity(nc, ident[:])
-
+        ident_bf = const.tile([P, P], BF16, name="ident_bf")
         w_raw = const.tile([P, 4, F], BF16, name="w_raw")
         pos = const.tile([P, 8, F], BF16, name="pos")
-        enc_sb = [const.tile([P, 2, 1024], BF16, name="enc%d" % c) for c in range(4)]
-
-        def load_w(h):
-            nc.sync.dma_start(out=w_raw[:, 2 * h:2 * h + 2, :].rearrange("s c f -> s (c f)"),
-                              in_=w_v[h])
-
-        def load_enc(c):
-            i, h = chunks[c]
-            for y in range(2):
-                nc.sync.dma_start(out=enc_sb[c][:, y, :],
-                                  in_=enc_v[i][:, :, y, h * 1024:(h + 1) * 1024])
-
-        def load_pos(h):
-            nc.sync.dma_start(out=pos[:, 4 * h:4 * h + 4, :], in_=pos_v[:, 4 * h:4 * h + 4, :])
-
-        load_w(0)
-        nc.sync.dma_start(out=brow[0:1, :], in_=b.rearrange("(o f) -> o f", o=1))
-        load_w(1)
-        load_enc(0)
-        load_pos(0)
-        load_enc(1)
-        load_pos(1)
-        load_enc(2)
-        load_enc(3)
-
+        posb = const.tile([P, 8, F], F32, name="posb")
+        bbc = const.tile([P, F], BF16, name="bbc")
         w_grp = const.tile([P, F, 4], BF16, name="w_grp", align_bytes=64)
         w_codes = const.tile([P, F], U32, name="w_codes", align_bytes=64)
         w_scales = const.tile([P, F], U8, name="w_scales", align_bytes=64)
-        bbc = const.tile([P, F], BF16, name="bbc")
-        pb = ps_t.tile([P, F], F32, name="pb", tag="t")
-        nc.tensor.matmul(out=pb[:], lhsT=ones[:], rhs=brow[:], start=True, stop=True)
-        nc.scalar.copy(out=bbc[:], in_=pb[:])
-
-        def regroup_w(copy, c0, c1):
-            copy(out=w_grp[:, c0:c1, :].rearrange("p (c i) t -> p c t i", i=4),
-                 in_=w_raw[:, :, c0:c1].rearrange("p t (c i) -> p c t i", i=4))
-
-        regroup_w(nc.scalar.copy, 336, 512)
-        regroup_w(nc.vector.tensor_copy, 0, 256)
-        regroup_w(nc.vector.tensor_copy, 256, 336)
-        for k in range(2):
-            nc.vector.quantize_mx(out=w_codes[:, k * 256:(k + 1) * 256].bitcast(FP8X4),
-                                  scales=w_scales[:, k * 256:(k + 1) * 256],
-                                  in_=w_grp[:, k * 256:(k + 1) * 256, :].rearrange("p f t -> p (f t)"))
-
-        posb = const.tile([P, 8, F], F32, name="posb")
-
-        def add_bias(eng, x):
-            eng.tensor_tensor(out=posb[:, x, :], in0=pos[:, x, :], in1=bbc[:], op=ADD)
-
-        for x in range(1, 8):
-            add_bias(nc.gpsimd, x)
-
+        enc_sb = [const.tile([P, 2, 1024], BF16, name="enc%d" % c) for c in range(4)]
+        ord_sb = [const.tile([P, 1024], F32, name="ord%d" % c) for c in range(4)]
         grp = [const.tile([P, 2048], BF16, name="grp%d" % c, align_bytes=64) for c in range(4)]
         codes = [const.tile([P, F], U32, name="codes%d" % c, align_bytes=64) for c in range(4)]
         scales = [const.tile([P, F], U8, name="scales%d" % c, align_bytes=64) for c in range(4)]
         res = [const.tile([P, 4, F], F32, name="res%d" % c) for c in range(4)]
 
-        ord_sb = [const.tile([P, 1024], F32, name="ord%d" % c) for c in range(4)]
+        def load_w(h):
+            nc.sync.dma_start(out=w_raw[:, 2 * h:2 * h + 2, :].rearrange("s c f -> s (c f)"),
+                              in_=w_v[h])
+
+        def load_enc(c, y):
+            i, h = chunks[c]
+            nc.sync.dma_start(out=enc_sb[c][:, y, :],
+                              in_=enc_v[i][:, :, y, h * 1024:(h + 1) * 1024])
+
+        def load_pos(x):
+            nc.sync.dma_start(out=pos[:, x:x + 2, :], in_=pos_v[:, x:x + 2, :])
+
+        nc.vector.memset(brow[:].bitcast(F32), 0.0)
+        nc.vector.memset(ones[:], 1.0)
+        make_identity(nc, ident[:])
+        load_enc(0, 0)
+        nc.sync.dma_start(out=brow[0:1, :], in_=b.rearrange("(o f) -> o f", o=1))
+        load_enc(0, 1)
+        load_w(0)
+        load_w(1)
+        load_pos(0)
+        load_pos(2)
+        load_enc(1, 0)
+        load_enc(1, 1)
+        load_enc(2, 0)
+        load_enc(2, 1)
+        load_pos(4)
+        load_pos(6)
+        load_enc(3, 0)
+        load_enc(3, 1)
+        nc.vector.tensor_copy(out=ident_bf[:], in_=ident[:])
 
         def reorder(u, copy):
             c, bank = u // 2, u % 2
@@ -105,7 +85,7 @@ def tile_resampling_kernel(tc, encoded, W, b, pos_emb, out):
                  in_=enc_sb[c][:].bitcast(F32)[:, :, bank * 256:(bank + 1) * 256]
                  .rearrange("p y (u w) -> p u y w", u=4))
 
-        def transpose_unit(u):
+        def transposes(u):
             c, bank = u // 2, u % 2
             pt = ps_t.tile([P, F], F32, name="pt", tag="t")
             for s in range(4):
@@ -120,11 +100,6 @@ def tile_resampling_kernel(tc, encoded, W, b, pos_emb, out):
                 .rearrange("p (x q h) -> p x q h", x=2, h=2),
                 in_=pt[:].rearrange("p (x h q) -> p x q h", x=2, h=2))
 
-        def transpose_pair(u):
-            banks = [transpose_unit(u), transpose_unit(u + 1)]
-            evacuate(u, banks[0])
-            evacuate(u + 1, banks[1])
-
         def quantise(u):
             c, bank = u // 2, u % 2
             nc.vector.quantize_mx(
@@ -132,6 +107,15 @@ def tile_resampling_kernel(tc, encoded, W, b, pos_emb, out):
                 scales=scales[c][:, bank * 256:(bank + 1) * 256],
                 in_=grp[c][:, bank * 1024:(bank + 1) * 1024],
             )
+
+        def regroup_w(copy, c0, c1):
+            copy(out=w_grp[:, c0:c1, :].rearrange("p (c i) t -> p c t i", i=4),
+                 in_=w_raw[:, :, c0:c1].rearrange("p t (c i) -> p c t i", i=4))
+
+        def quantise_w(k):
+            nc.vector.quantize_mx(out=w_codes[:, k * 256:(k + 1) * 256].bitcast(FP8X4),
+                                  scales=w_scales[:, k * 256:(k + 1) * 256],
+                                  in_=w_grp[:, k * 256:(k + 1) * 256, :].rearrange("p f t -> p (f t)"))
 
         def mx_pass(n):
             c, xi = n // 4, n % 4
@@ -154,33 +138,44 @@ def tile_resampling_kernel(tc, encoded, W, b, pos_emb, out):
                                     op=ADD)
             nc.sync.dma_start(out=out_v[i][:, h * 4 + xi, :], in_=res[c][:, xi, :])
 
-        def finish_unit(u, acc):
-            finish(2 * u, acc[0])
-            finish(2 * u + 1, acc[1])
-            if u + 2 < 8:
-                quantise(u + 2)
+        def posb_on_pe(x):
+            pb = ps_o.tile([P, F], F32, name="pb", tag="o")
+            nc.tensor.matmul(out=pb[:], lhsT=ident_bf[:], rhs=pos[:, x, :], start=True, stop=False)
+            nc.tensor.matmul(out=pb[:], lhsT=ones[:], rhs=brow[:], start=False, stop=True)
+            return pb
 
+        pb = ps_o.tile([P, F], F32, name="pbb", tag="o")
+        nc.tensor.matmul(out=pb[:], lhsT=ones[:], rhs=brow[:], start=True, stop=True)
+        nc.scalar.copy(out=bbc[:], in_=pb[:])
         reorder(0, nc.vector.tensor_copy)
         reorder(1, nc.vector.tensor_copy)
-        transpose_pair(0)
-        reorder(2, nc.scalar.copy)
-        reorder(3, nc.scalar.copy)
+        pt = [transposes(0), transposes(1)]
+        regroup_w(nc.scalar.copy, 384, 512)
+        evacuate(0, pt[0])
+        evacuate(1, pt[1])
+        regroup_w(nc.vector.tensor_copy, 0, 256)
+        regroup_w(nc.vector.tensor_copy, 256, 384)
+        quantise_w(0)
+        quantise_w(1)
         quantise(0)
-        add_bias(nc.vector, 0)
         quantise(1)
-        first = [mx_pass(0), mx_pass(1)]
-        transpose_pair(2)
-        reorder(4, nc.scalar.copy)
-        reorder(5, nc.scalar.copy)
-        second = [mx_pass(2), mx_pass(3)]
-        finish_unit(0, first)
-        finish_unit(1, second)
-        for g in range(1, 4):
-            if g < 3:
-                transpose_pair(2 * g + 2)
-                if g < 2:
-                    reorder(6, nc.scalar.copy)
-                    reorder(7, nc.scalar.copy)
-            acc = [mx_pass(4 * g + k) for k in range(4)]
-            finish_unit(2 * g, acc[0:2])
-            finish_unit(2 * g + 1, acc[2:4])
+        pb0 = posb_on_pe(0)
+        pb1 = posb_on_pe(1)
+        for x in range(2, 8):
+            nc.gpsimd.tensor_tensor(out=posb[:, x, :], in0=pos[:, x, :], in1=bbc[:], op=ADD)
+        nc.scalar.copy(out=posb[:, 0, :], in_=pb0[:])
+        nc.scalar.copy(out=posb[:, 1, :], in_=pb1[:])
+        reorder(2, nc.scalar.copy)
+
+        for u in range(8):
+            a0 = mx_pass(2 * u)
+            a1 = mx_pass(2 * u + 1)
+            if u + 3 < 8:
+                reorder(u + 3, nc.scalar.copy)
+            if u + 2 < 8:
+                pt = transposes(u + 2)
+                evacuate(u + 2, pt)
+            if 1 <= u < 7:
+                quantise(u + 1)
+            finish(2 * u, a0)
+            finish(2 * u + 1, a1)

@@ -68,9 +68,9 @@ def tile_resampling_kernel(tc, encoded, W, b, pos_emb, out):
         load_w(0)
         load_w(1)
         load_pos(0)
-        load_pos(2)
         load_enc(1, 0)
         load_enc(1, 1)
+        load_pos(2)
         load_enc(2, 0)
         load_enc(2, 1)
         load_pos(4)
@@ -159,18 +159,19 @@ def tile_resampling_kernel(tc, encoded, W, b, pos_emb, out):
         quantise_w(1)
         quantise(0)
         quantise(1)
+        reorder(2, nc.vector.tensor_copy)
+        reorder(3, nc.vector.tensor_copy)
         pb0 = posb_on_pe(0)
         pb1 = posb_on_pe(1)
         for x in range(2, 8):
             nc.gpsimd.tensor_tensor(out=posb[:, x, :], in0=pos[:, x, :], in1=bbc[:], op=ADD)
         nc.scalar.copy(out=posb[:, 0, :], in_=pb0[:])
         nc.scalar.copy(out=posb[:, 1, :], in_=pb1[:])
-        reorder(2, nc.scalar.copy)
 
         for u in range(8):
             a0 = mx_pass(2 * u)
             a1 = mx_pass(2 * u + 1)
-            if u + 3 < 8:
+            if 4 <= u + 3 < 8:
                 reorder(u + 3, nc.scalar.copy)
             if u + 2 < 8:
                 pt = transposes(u + 2)

@@ -29,20 +29,20 @@ def tile_resampling_kernel(tc, encoded, W, b, pos_emb, out):
         out_v = out.rearrange("i (m x) f -> i m x f", x=8)
         chunks = [(0, 0), (1, 0), (0, 1), (1, 1)]
 
-        brow = const.tile([P, F], BF16, name="brow")
-        ones = const.tile([P, P], BF16, name="ones")
+        b_col = const.tile([P, 4], BF16, name="b_col")
         ident = const.tile([P, P], F32, name="ident")
         ident_bf = const.tile([P, P], BF16, name="ident_bf")
         w_raw = const.tile([P, 4, F], BF16, name="w_raw")
         pos = const.tile([P, 8, F], BF16, name="pos")
-        posb = const.tile([P, 8, F], F32, name="posb")
         bbc = const.tile([P, F], BF16, name="bbc")
         w_grp = const.tile([P, F, 4], BF16, name="w_grp", align_bytes=64)
         w_codes = const.tile([P, F], U32, name="w_codes", align_bytes=64)
         w_scales = const.tile([P, F], U8, name="w_scales", align_bytes=64)
         enc_sb = [const.tile([P, 2, 1024], BF16, name="enc%d" % c) for c in range(4)]
         ord_sb = [const.tile([P, 1024], F32, name="ord%d" % c) for c in range(4)]
-        grp = [const.tile([P, 2048], BF16, name="grp%d" % c, align_bytes=64) for c in range(4)]
+        grp = [const.tile([P, 1024], BF16, name="grp%d" % u, align_bytes=64) for u in range(8)]
+        posb = [const.tile([P, F], F32, name="posb%d" % x)[:] for x in range(3)]
+        posb += [enc_sb[1][:, 0, :].bitcast(F32)] + [grp[u][:].bitcast(F32) for u in range(2, 6)]
         codes = [const.tile([P, F], U32, name="codes%d" % c, align_bytes=64) for c in range(4)]
         scales = [const.tile([P, F], U8, name="scales%d" % c, align_bytes=64) for c in range(4)]
         res = [const.tile([P, 4, F], F32, name="res%d" % c) for c in range(4)]
@@ -59,11 +59,9 @@ def tile_resampling_kernel(tc, encoded, W, b, pos_emb, out):
         def load_pos(x):
             nc.sync.dma_start(out=pos[:, x:x + 2, :], in_=pos_v[:, x:x + 2, :])
 
-        nc.vector.memset(brow[:].bitcast(F32), 0.0)
-        nc.vector.memset(ones[:], 1.0)
         make_identity(nc, ident[:])
         load_enc(0, 0)
-        nc.sync.dma_start(out=brow[0:1, :], in_=b.rearrange("(o f) -> o f", o=1))
+        nc.sync.dma_start(out=b_col[:], in_=b.rearrange("(p t) -> p t", t=4))
         load_enc(0, 1)
         load_w(0)
         load_w(1)
@@ -94,9 +92,8 @@ def tile_resampling_kernel(tc, encoded, W, b, pos_emb, out):
             return pt
 
         def evacuate(u, pt):
-            c, bank = u // 2, u % 2
             nc.scalar.copy(
-                out=grp[c][:].bitcast(F32)[:, bank * F:(bank + 1) * F]
+                out=grp[u][:].bitcast(F32)
                 .rearrange("p (x q h) -> p x q h", x=2, h=2),
                 in_=pt[:].rearrange("p (x h q) -> p x q h", x=2, h=2))
 
@@ -105,7 +102,7 @@ def tile_resampling_kernel(tc, encoded, W, b, pos_emb, out):
             nc.vector.quantize_mx(
                 out=codes[c][:, bank * 256:(bank + 1) * 256].bitcast(FP8X4),
                 scales=scales[c][:, bank * 256:(bank + 1) * 256],
-                in_=grp[c][:, bank * 1024:(bank + 1) * 1024],
+                in_=grp[u][:],
             )
 
         def regroup_w(copy, c0, c1):
@@ -134,19 +131,25 @@ def tile_resampling_kernel(tc, encoded, W, b, pos_emb, out):
         def finish(n, po):
             c, xi = n // 4, n % 4
             i, h = chunks[c]
-            nc.vector.tensor_tensor(out=res[c][:, xi, :], in0=po[:], in1=posb[:, h * 4 + xi, :],
+            nc.vector.tensor_tensor(out=res[c][:, xi, :], in0=po[:], in1=posb[h * 4 + xi],
                                     op=ADD)
             nc.sync.dma_start(out=out_v[i][:, h * 4 + xi, :], in_=res[c][:, xi, :])
+
+        def add_bias(x):
+            nc.gpsimd.tensor_tensor(out=posb[x], in0=pos[:, x, :], in1=bbc[:], op=ADD)
 
         def posb_on_pe(x):
             pb = ps_o.tile([P, F], F32, name="pb", tag="o")
             nc.tensor.matmul(out=pb[:], lhsT=ident_bf[:], rhs=pos[:, x, :], start=True, stop=False)
-            nc.tensor.matmul(out=pb[:], lhsT=ones[:], rhs=brow[:], start=False, stop=True)
+            nc.tensor.matmul(out=pb[:], lhsT=ident_bf[:], rhs=bbc[:], start=False, stop=True)
             return pb
 
-        pb = ps_o.tile([P, F], F32, name="pbb", tag="o")
-        nc.tensor.matmul(out=pb[:], lhsT=ones[:], rhs=brow[:], start=True, stop=True)
-        nc.scalar.copy(out=bbc[:], in_=pb[:])
+        pb = ps_o.tile([P, F], BF16, name="pbb", tag="o")
+        for t in range(4):
+            nc.tensor.transpose(pb[:, t * P:(t + 1) * P], b_col[:, t:t + 1].to_broadcast([P, P]),
+                                ident_bf[:])
+        nc.scalar.copy(out=bbc[:].rearrange("p (f t) -> p f t", t=4),
+                       in_=pb[:].rearrange("p (t f) -> p f t", t=4))
         reorder(0, nc.vector.tensor_copy)
         reorder(1, nc.vector.tensor_copy)
         pt = [transposes(0), transposes(1)]
@@ -163,10 +166,9 @@ def tile_resampling_kernel(tc, encoded, W, b, pos_emb, out):
         reorder(3, nc.vector.tensor_copy)
         pb0 = posb_on_pe(0)
         pb1 = posb_on_pe(1)
-        for x in range(2, 8):
-            nc.gpsimd.tensor_tensor(out=posb[:, x, :], in0=pos[:, x, :], in1=bbc[:], op=ADD)
-        nc.scalar.copy(out=posb[:, 0, :], in_=pb0[:])
-        nc.scalar.copy(out=posb[:, 1, :], in_=pb1[:])
+        add_bias(3)
+        nc.scalar.copy(out=posb[0], in_=pb0[:])
+        nc.scalar.copy(out=posb[1], in_=pb1[:])
 
         for u in range(8):
             a0 = mx_pass(2 * u)
@@ -178,5 +180,10 @@ def tile_resampling_kernel(tc, encoded, W, b, pos_emb, out):
                 evacuate(u + 2, pt)
             if 1 <= u < 7:
                 quantise(u + 1)
+                if u < 5:
+                    add_bias(u + 3)
             finish(2 * u, a0)
+            if u == 0:
+                pb2 = posb_on_pe(2)
+                nc.scalar.copy(out=posb[2], in_=pb2[:])
             finish(2 * u + 1, a1)

@@ -131,9 +131,14 @@ def tile_resampling_kernel(tc, encoded, W, b, pos_emb, out):
         def finish(n, po):
             c, xi = n // 4, n % 4
             i, h = chunks[c]
+            u = n // 2
             nc.vector.tensor_tensor(out=res[c][:, xi, :], in0=po[:], in1=posb[h * 4 + xi],
                                     op=ADD)
-            nc.sync.dma_start(out=out_v[i][:, h * 4 + xi, :], in_=res[c][:, xi, :])
+            if u == 7:
+                nc.sync.dma_start(out=out_v[i][:, h * 4 + xi, :], in_=res[c][:, xi, :])
+            elif xi % 2 == 1:
+                nc.sync.dma_start(out=out_v[i][:, h * 4 + xi - 1:h * 4 + xi + 1, :],
+                                  in_=res[c][:, xi - 1:xi + 1, :])
 
         def add_bias(x):
             nc.gpsimd.tensor_tensor(out=posb[x], in0=pos[:, x, :], in1=bbc[:], op=ADD)

@@ -41,8 +41,8 @@ def tile_resampling_kernel(tc, encoded, W, b, pos_emb, out):
         enc_sb = [const.tile([P, 2, 1024], BF16, name="enc%d" % c) for c in range(4)]
         ord_sb = [const.tile([P, 1024], F32, name="ord%d" % c) for c in range(4)]
         grp = [const.tile([P, 1024], BF16, name="grp%d" % u, align_bytes=64) for u in range(8)]
-        posb = [const.tile([P, F], F32, name="posb%d" % x)[:] for x in range(3)]
-        posb += [enc_sb[1][:, 0, :].bitcast(F32)] + [grp[u][:].bitcast(F32) for u in range(2, 6)]
+        posb = [const.tile([P, F], F32, name="posb%d" % x)[:] for x in range(4)]
+        posb += [grp[2][:].bitcast(F32), grp[3][:].bitcast(F32), posb[1], posb[3]]
         codes = [const.tile([P, F], U32, name="codes%d" % c, align_bytes=64) for c in range(4)]
         scales = [const.tile([P, F], U8, name="scales%d" % c, align_bytes=64) for c in range(4)]
         res = [const.tile([P, 4, F], F32, name="res%d" % c) for c in range(4)]
@@ -71,8 +71,7 @@ def tile_resampling_kernel(tc, encoded, W, b, pos_emb, out):
         load_pos(2)
         load_enc(2, 0)
         load_enc(2, 1)
-        load_pos(4)
-        load_pos(6)
+        nc.sync.dma_start(out=pos[:, 4:8, :], in_=pos_v[:, 4:8, :])
         load_enc(3, 0)
         load_enc(3, 1)
         nc.vector.tensor_copy(out=ident_bf[:], in_=ident[:])
@@ -131,17 +130,16 @@ def tile_resampling_kernel(tc, encoded, W, b, pos_emb, out):
         def finish(n, po):
             c, xi = n // 4, n % 4
             i, h = chunks[c]
-            u = n // 2
             nc.vector.tensor_tensor(out=res[c][:, xi, :], in0=po[:], in1=posb[h * 4 + xi],
                                     op=ADD)
-            if u == 7:
+            if n >= 10:
                 nc.sync.dma_start(out=out_v[i][:, h * 4 + xi, :], in_=res[c][:, xi, :])
             elif xi % 2 == 1:
                 nc.sync.dma_start(out=out_v[i][:, h * 4 + xi - 1:h * 4 + xi + 1, :],
                                   in_=res[c][:, xi - 1:xi + 1, :])
 
-        def add_bias(x):
-            nc.gpsimd.tensor_tensor(out=posb[x], in0=pos[:, x, :], in1=bbc[:], op=ADD)
+        def add_bias(x, eng=nc.gpsimd):
+            eng.tensor_tensor(out=posb[x], in0=pos[:, x, :], in1=bbc[:], op=ADD)
 
         def posb_on_pe(x):
             pb = ps_o.tile([P, F], F32, name="pb", tag="o")
@@ -166,14 +164,13 @@ def tile_resampling_kernel(tc, encoded, W, b, pos_emb, out):
         quantise_w(0)
         quantise_w(1)
         quantise(0)
+        add_bias(0, nc.vector)
         quantise(1)
         reorder(2, nc.vector.tensor_copy)
-        reorder(3, nc.vector.tensor_copy)
-        pb0 = posb_on_pe(0)
         pb1 = posb_on_pe(1)
-        add_bias(3)
-        nc.scalar.copy(out=posb[0], in_=pb0[:])
         nc.scalar.copy(out=posb[1], in_=pb1[:])
+        reorder(3, nc.scalar.copy)
+        add_bias(2)
 
         for u in range(8):
             a0 = mx_pass(2 * u)
@@ -185,10 +182,12 @@ def tile_resampling_kernel(tc, encoded, W, b, pos_emb, out):
                 evacuate(u + 2, pt)
             if 1 <= u < 7:
                 quantise(u + 1)
-                if u < 5:
+                if u < 3:
                     add_bias(u + 3)
             finish(2 * u, a0)
             if u == 0:
-                pb2 = posb_on_pe(2)
-                nc.scalar.copy(out=posb[2], in_=pb2[:])
+                pb3 = posb_on_pe(3)
+                nc.scalar.copy(out=posb[3], in_=pb3[:])
             finish(2 * u + 1, a1)
+            if u in (2, 3):
+                add_bias(u + 4)

@@ -29,7 +29,8 @@ def tile_resampling_kernel(tc, encoded, W, b, pos_emb, out):
         out_v = out.rearrange("i (m x) f -> i m x f", x=8)
         chunks = [(0, 0), (1, 0), (0, 1), (1, 1)]
 
-        b_col = const.tile([P, 4], BF16, name="b_col")
+        brow = const.tile([P, F], BF16, name="brow")
+        ones = const.tile([P, P], BF16, name="ones")
         ident = const.tile([P, P], F32, name="ident")
         ident_bf = const.tile([P, P], BF16, name="ident_bf")
         w_raw = const.tile([P, 4, F], BF16, name="w_raw")
@@ -42,6 +43,7 @@ def tile_resampling_kernel(tc, encoded, W, b, pos_emb, out):
         ord_sb = [const.tile([P, 1024], F32, name="ord%d" % c) for c in range(4)]
         grp = [const.tile([P, 1024], BF16, name="grp%d" % u, align_bytes=64) for u in range(8)]
         posb = [const.tile([P, F], F32, name="posb%d" % x)[:] for x in range(4)]
+        posb[2] = grp[1][:].bitcast(F32)
         posb += [grp[2][:].bitcast(F32), grp[3][:].bitcast(F32), posb[1], posb[3]]
         codes = [const.tile([P, F], U32, name="codes%d" % c, align_bytes=64) for c in range(4)]
         scales = [const.tile([P, F], U8, name="scales%d" % c, align_bytes=64) for c in range(4)]
@@ -60,8 +62,10 @@ def tile_resampling_kernel(tc, encoded, W, b, pos_emb, out):
             nc.sync.dma_start(out=pos[:, x:x + 2, :], in_=pos_v[:, x:x + 2, :])
 
         make_identity(nc, ident[:])
+        nc.vector.memset(brow[:].bitcast(F32), 0.0)
+        nc.vector.memset(ones[:], 1.0)
         load_enc(0, 0)
-        nc.sync.dma_start(out=b_col[:], in_=b.rearrange("(p t) -> p t", t=4))
+        nc.sync.dma_start(out=brow[0:1, :], in_=b.rearrange("(o f) -> o f", o=1))
         load_enc(0, 1)
         load_w(0)
         load_w(1)
@@ -71,7 +75,8 @@ def tile_resampling_kernel(tc, encoded, W, b, pos_emb, out):
         load_pos(2)
         load_enc(2, 0)
         load_enc(2, 1)
-        nc.sync.dma_start(out=pos[:, 4:8, :], in_=pos_v[:, 4:8, :])
+        load_pos(4)
+        load_pos(6)
         load_enc(3, 0)
         load_enc(3, 1)
         nc.vector.tensor_copy(out=ident_bf[:], in_=ident[:])
@@ -132,7 +137,7 @@ def tile_resampling_kernel(tc, encoded, W, b, pos_emb, out):
             i, h = chunks[c]
             nc.vector.tensor_tensor(out=res[c][:, xi, :], in0=po[:], in1=posb[h * 4 + xi],
                                     op=ADD)
-            if n >= 10:
+            if n >= 8:
                 nc.sync.dma_start(out=out_v[i][:, h * 4 + xi, :], in_=res[c][:, xi, :])
             elif xi % 2 == 1:
                 nc.sync.dma_start(out=out_v[i][:, h * 4 + xi - 1:h * 4 + xi + 1, :],
@@ -144,15 +149,12 @@ def tile_resampling_kernel(tc, encoded, W, b, pos_emb, out):
         def posb_on_pe(x):
             pb = ps_o.tile([P, F], F32, name="pb", tag="o")
             nc.tensor.matmul(out=pb[:], lhsT=ident_bf[:], rhs=pos[:, x, :], start=True, stop=False)
-            nc.tensor.matmul(out=pb[:], lhsT=ident_bf[:], rhs=bbc[:], start=False, stop=True)
+            nc.tensor.matmul(out=pb[:], lhsT=ones[:], rhs=brow[:], start=False, stop=True)
             return pb
 
-        pb = ps_o.tile([P, F], BF16, name="pbb", tag="o")
-        for t in range(4):
-            nc.tensor.transpose(pb[:, t * P:(t + 1) * P], b_col[:, t:t + 1].to_broadcast([P, P]),
-                                ident_bf[:])
-        nc.scalar.copy(out=bbc[:].rearrange("p (f t) -> p f t", t=4),
-                       in_=pb[:].rearrange("p (t f) -> p f t", t=4))
+        pb = ps_o.tile([P, F], F32, name="pbb", tag="o")
+        nc.tensor.matmul(out=pb[:], lhsT=ones[:], rhs=brow[:], start=True, stop=True)
+        nc.scalar.copy(out=bbc[:], in_=pb[:])
         reorder(0, nc.vector.tensor_copy)
         reorder(1, nc.vector.tensor_copy)
         pt = [transposes(0), transposes(1)]

@@ -167,8 +167,8 @@ def tile_resampling_kernel(tc, encoded, W, b, pos_emb, out):
         quantise_w(1)
         quantise(0)
         add_bias(0, nc.vector)
-        quantise(1)
         reorder(2, nc.vector.tensor_copy)
+        quantise(1)
         pb1 = posb_on_pe(1)
         nc.scalar.copy(out=posb[1], in_=pb1[:])
         reorder(3, nc.scalar.copy)

from contextlib import ExitStack

import concourse.mybir as mybir
from concourse.masks import make_identity

F32 = mybir.dt.float32
BF16 = mybir.dt.bfloat16
U32 = mybir.dt.uint32
U8 = mybir.dt.uint8
FP8X4 = mybir.dt.float8_e4m3fn_x4
ADD = mybir.AluOpType.add

P = 128
F = 512
FLOPS = 2 * 2048 * 512 * 512


def tile_resampling_kernel(tc, encoded, W, b, pos_emb, out):
    nc = tc.nc
    with ExitStack() as ctx:
        const = ctx.enter_context(tc.tile_pool(name="const", bufs=1))
        ps_t = ctx.enter_context(tc.psum_pool(name="ps_t", bufs=3))
        ps_o = ctx.enter_context(tc.psum_pool(name="ps_o", bufs=5))
        ctx.enter_context(tc.manual_schedule())

        enc_v = encoded.rearrange("i (Y y C c) d -> i Y C y (c d)", Y=32, y=2, C=4)
        w_v = W.rearrange("(y h w e) f -> h y w (e f)", y=16, h=2, w=8, e=2)
        pos_v = pos_emb.rearrange("(m x) f -> m x f", x=8)
        out_v = out.rearrange("i (m x) f -> i m x f", x=8)
        chunks = [(0, 0), (1, 0), (0, 1), (1, 1)]

        brow = const.tile([P, F], BF16, name="brow")
        ones = const.tile([P, P], BF16, name="ones")
        ident = const.tile([P, P], F32, name="ident")
        ident_bf = const.tile([P, P], BF16, name="ident_bf")
        w_raw = const.tile([P, 4, F], BF16, name="w_raw")
        pos = const.tile([P, 8, F], BF16, name="pos")
        bbc = const.tile([P, F], BF16, name="bbc")
        w_grp = const.tile([P, F, 4], BF16, name="w_grp", align_bytes=64)
        w_codes = const.tile([P, F], U32, name="w_codes", align_bytes=64)
        w_scales = const.tile([P, F], U8, name="w_scales", align_bytes=64)
        enc_sb = [const.tile([P, 2, 1024], BF16, name="enc%d" % c) for c in range(4)]
        ord_sb = [const.tile([P, 1024], F32, name="ord%d" % c) for c in range(4)]
        grp = [const.tile([P, 1024], BF16, name="grp%d" % u, align_bytes=64) for u in range(8)]
        posb = [const.tile([P, F], F32, name="posb%d" % x)[:] for x in range(4)]
        posb[2] = grp[1][:].bitcast(F32)
        posb += [grp[2][:].bitcast(F32), grp[3][:].bitcast(F32), posb[1], posb[3]]
        codes = [const.tile([P, F], U32, name="codes%d" % c, align_bytes=64) for c in range(4)]
        scales = [const.tile([P, F], U8, name="scales%d" % c, align_bytes=64) for c in range(4)]
        res = [const.tile([P, 4, F], F32, name="res%d" % c) for c in range(4)]

        def load_w(h):
            nc.sync.dma_start(out=w_raw[:, 2 * h:2 * h + 2, :].rearrange("s c f -> s (c f)"),
                              in_=w_v[h])

        def load_enc(c, y):
            i, h = chunks[c]
            nc.sync.dma_start(out=enc_sb[c][:, y, :],
                              in_=enc_v[i][:, :, y, h * 1024:(h + 1) * 1024])

        def load_pos(x):
            nc.sync.dma_start(out=pos[:, x:x + 2, :], in_=pos_v[:, x:x + 2, :])

        make_identity(nc, ident[:])
        nc.vector.memset(brow[:].bitcast(F32), 0.0)
        nc.vector.memset(ones[:], 1.0)
        load_enc(0, 0)
        nc.sync.dma_start(out=brow[0:1, :], in_=b.rearrange("(o f) -> o f", o=1))
        load_enc(0, 1)
        load_w(0)
        load_w(1)
        load_pos(0)
        load_enc(1, 0)
        load_enc(1, 1)
        load_pos(2)
        load_enc(2, 0)
        load_enc(2, 1)
        load_pos(4)
        load_pos(6)
        load_enc(3, 0)
        load_enc(3, 1)
        nc.vector.tensor_copy(out=ident_bf[:], in_=ident[:])

        def reorder(u, copy):
            c, bank = u // 2, u % 2
            copy(out=ord_sb[c][:, bank * F:(bank + 1) * F].rearrange("p (u y w) -> p u y w", u=4, y=2),
                 in_=enc_sb[c][:].bitcast(F32)[:, :, bank * 256:(bank + 1) * 256]
                 .rearrange("p y (u w) -> p u y w", u=4))

        def transposes(u):
            c, bank = u // 2, u % 2
            pt = ps_t.tile([P, F], F32, name="pt", tag="t")
            for s in range(4):
                nc.tensor.transpose(pt[:, s * P:(s + 1) * P],
                                    ord_sb[c][:, (4 * bank + s) * P:(4 * bank + s + 1) * P], ident[:])
            return pt

        def evacuate(u, pt):
            nc.scalar.copy(
                out=grp[u][:].bitcast(F32)
                .rearrange("p (x q h) -> p x q h", x=2, h=2),
                in_=pt[:].rearrange("p (x h q) -> p x q h", x=2, h=2))

        def quantise(u):
            c, bank = u // 2, u % 2
            nc.vector.quantize_mx(
                out=codes[c][:, bank * 256:(bank + 1) * 256].bitcast(FP8X4),
                scales=scales[c][:, bank * 256:(bank + 1) * 256],
                in_=grp[u][:],
            )

        def regroup_w(copy, c0, c1):
            copy(out=w_grp[:, c0:c1, :].rearrange("p (c i) t -> p c t i", i=4),
                 in_=w_raw[:, :, c0:c1].rearrange("p t (c i) -> p c t i", i=4))

        def quantise_w(k):
            nc.vector.quantize_mx(out=w_codes[:, k * 256:(k + 1) * 256].bitcast(FP8X4),
                                  scales=w_scales[:, k * 256:(k + 1) * 256],
                                  in_=w_grp[:, k * 256:(k + 1) * 256, :].rearrange("p f t -> p (f t)"))

        def mx_pass(n):
            c, xi = n // 4, n % 4
            po = ps_o.tile([P, F], F32, name="po", tag="o")
            nc.tensor.matmul_mx(
                out=po[:],
                lhsT=codes[c][:, xi * P:(xi + 1) * P].bitcast(FP8X4),
                lhsT_scale=scales[c][:, xi * P:(xi + 1) * P],
                rhs=w_codes[:].bitcast(FP8X4),
                rhs_scale=w_scales[:],
                start=True,
                stop=True,
            )
            return po

        def finish(n, po):
            c, xi = n // 4, n % 4
            i, h = chunks[c]
            nc.vector.tensor_tensor(out=res[c][:, xi, :], in0=po[:], in1=posb[h * 4 + xi],
                                    op=ADD)
            if n >= 8:
                nc.sync.dma_start(out=out_v[i][:, h * 4 + xi, :], in_=res[c][:, xi, :])
            elif xi % 2 == 1:
                nc.sync.dma_start(out=out_v[i][:, h * 4 + xi - 1:h * 4 + xi + 1, :],
                                  in_=res[c][:, xi - 1:xi + 1, :])

        def add_bias(x, eng=nc.gpsimd):
            eng.tensor_tensor(out=posb[x], in0=pos[:, x, :], in1=bbc[:], op=ADD)

        def posb_on_pe(x):
            pb = ps_o.tile([P, F], F32, name="pb", tag="o")
            nc.tensor.matmul(out=pb[:], lhsT=ident_bf[:], rhs=pos[:, x, :], start=True, stop=False)
            nc.tensor.matmul(out=pb[:], lhsT=ones[:], rhs=brow[:], start=False, stop=True)
            return pb

        pb = ps_o.tile([P, F], F32, name="pbb", tag="o")
        nc.tensor.matmul(out=pb[:], lhsT=ones[:], rhs=brow[:], start=True, stop=True)
        nc.scalar.copy(out=bbc[:], in_=pb[:])
        reorder(0, nc.vector.tensor_copy)
        reorder(1, nc.vector.tensor_copy)
        pt = [transposes(0), transposes(1)]
        regroup_w(nc.scalar.copy, 384, 512)
        evacuate(0, pt[0])
        evacuate(1, pt[1])
        regroup_w(nc.vector.tensor_copy, 0, 256)
        regroup_w(nc.vector.tensor_copy, 256, 384)
        quantise_w(0)
        quantise_w(1)
        quantise(0)
        add_bias(0, nc.vector)
        reorder(2, nc.vector.tensor_copy)
        quantise(1)
        pb1 = posb_on_pe(1)
        nc.scalar.copy(out=posb[1], in_=pb1[:])
        reorder(3, nc.scalar.copy)
        add_bias(2)

        for u in range(8):
            a0 = mx_pass(2 * u)
            a1 = mx_pass(2 * u + 1)
            if 4 <= u + 3 < 8:
                reorder(u + 3, nc.scalar.copy)
            if u + 2 < 8:
                pt = transposes(u + 2)
                evacuate(u + 2, pt)
            if 1 <= u < 7:
                quantise(u + 1)
                if u < 3:
                    add_bias(u + 3)
            finish(2 * u, a0)
            if u == 0:
                pb3 = posb_on_pe(3)
                nc.scalar.copy(out=posb[3], in_=pb3[:])
            finish(2 * u + 1, a1)
            if u in (2, 3):
                add_bias(u + 4)
